import numpy as np
import ml_dtypes


def mxq(x, axis, fmt="e4m3"):
    dtype, down = {"e4m3": (ml_dtypes.float8_e4m3fn, 7), "e5m2": (ml_dtypes.float8_e5m2, 14)}[fmt]
    v = np.moveaxis(np.asarray(x, np.float32).astype(ml_dtypes.bfloat16).astype(np.float64), axis, -1)
    blocks = v.reshape(v.shape[:-1] + (-1, 32))
    amax = np.abs(blocks).max(-1, keepdims=True)
    byte = np.maximum(np.where(amax > 0, np.frexp(amax)[1] - 1 + 127, 0) - down, 1)
    scale = np.exp2(byte - 127.0)
    codes = (blocks / scale).astype(np.float32).astype(dtype).astype(np.float64)
    return np.moveaxis((codes * scale).reshape(v.shape), -1, axis)


WIDE = False


def mx_kscale(k):
    if not WIDE:
        return np.ones(k)
    levels = np.array([10, -10, 5, -5, 0])
    a = np.random.permutation(np.resize(levels, k // 512 * 4)).reshape(k // 512, 4)
    idx = np.arange(k)
    return np.exp2(a[idx // 512, idx % 128 // 32])


BF16 = ml_dtypes.bfloat16


def bf(x):
    return np.asarray(x, np.float32).astype(BF16)


def f64(x):
    return np.asarray(x).astype(np.float64)


B, D, F, M, BLK = 8192, 7, 512, 256, 32
DP = D + 1
FUSED = DP * DP * DP
OS = 0.75
W1S = (1.0 + D * OS * OS / 2.0) ** -1.5


def wide_factors():
    s = mx_kscale(FUSED)
    if DP % BLK == 0:
        return np.ones(DP), np.append(s[::DP][:D], 1.0)
    return np.append(s[::DP * DP][:D], 1.0), np.ones(DP)


def stream():
    return np.maximum(np.random.standard_normal((B, D)) * OS, 0.0)


def setup_inputs():
    a, b = wide_factors()
    t = mx_kscale(F)
    col = (a[:, None, None] * b[None, :, None] * np.ones(DP)).reshape(FUSED)
    return {
        'o1': bf(stream() * a[:D]),
        'o2': bf(stream() * b[:D]),
        'o3': bf(stream()),
        'We1': bf(np.random.standard_normal((F, FUSED)) * W1S * t[:, None] / col),
        'be1': bf(np.random.standard_normal(F) * 0.2 * t),
        'We2': bf(np.random.standard_normal((M, F)) * np.sqrt(2.0 / F) / t),
        'be2': bf(np.random.standard_normal(M) * 0.2),
    }


def with_ones(o):
    return np.concatenate([o, np.ones((o.shape[0], 1))], axis=1)


def reference(o1, o2, o3, We1, be1, We2, be2):
    p1, p2, p3 = with_ones(f64(o1)), with_ones(f64(o2)), with_ones(f64(o3))
    o123 = (p1[:, :, None, None] * p2[:, None, :, None] * p3[:, None, None, :]).reshape(p1.shape[0], -1)
    h = np.maximum((mxq(o123, 1, 'e4m3') @ mxq(f64(We1), 1, 'e4m3').T) + f64(be1), 0.0)
    return np.maximum((mxq(h, 1, 'e4m3') @ mxq(f64(We2), 1, 'e4m3').T) + f64(be2), 0.0)

@@ -1,0 +1,281 @@
+from contextlib import ExitStack
+
+import concourse.bass as bass
+import concourse.mybir as mybir
+import concourse.tile as tile
+from concourse.masks import make_identity
+
+F32 = mybir.dt.float32
+BF16 = mybir.dt.bfloat16
+U32 = mybir.dt.uint32
+U8 = mybir.dt.uint8
+FP8X4 = mybir.dt.float8_e4m3fn_x4
+ALU = mybir.AluOpType
+ACT = mybir.ActivationFunctionType
+
+P = 128
+B = 8192
+D = 7
+F = 512
+M = 256
+CH = 512
+NCH = B // CH
+NT = B // P
+FLOPS = 2 * B * 512 * F + 2 * B * F * M
+SCR0 = B - 128
+G_GROUPS = [4, 5, 6, 7]
+TAIL = 15
+V_GROUPS = [(0, 1), (1, 2), (2, 4), (4, 8), (8, 12), (12, 16)]
+
+
+def tile_tensor_fusion_pa_t_kernel(tc, o1, o2, o3, We1, be1, We2, be2, out):
+    nc = tc.nc
+    with ExitStack() as ctx:
+        keep = ctx.enter_context(tc.tile_pool(name="keep", bufs=1))
+        work = ctx.enter_context(tc.tile_pool(name="work", bufs=2))
+        psum = ctx.enter_context(tc.psum_pool(name="psum", bufs=1))
+        ctx.enter_context(tc.manual_schedule())
+
+        o3_sb = keep.tile([P, NT, D], BF16)
+        o1_sb = keep.tile([P, NT, D], BF16)
+        o2_sb = keep.tile([P, NT, D], BF16)
+        for sb, dr in ((o3_sb, o3), (o1_sb, o1), (o2_sb, o2)):
+            nc.sync.dma_start(
+                out=sb[:].rearrange("p (c n) k -> p c (n k)", n=4),
+                in_=dr.rearrange("(c p n) k -> p c (n k)", p=P, n=4),
+            )
+        w1_sb = keep.tile([P, 4, 512], BF16)
+        nc.scalar.dma_start(out=w1_sb[:], in_=We1.rearrange("(q a) k -> q a k", a=4))
+        w2_sb = keep.tile([P, 2, 512], BF16)
+        nc.scalar.dma_start(out=w2_sb[:], in_=We2.rearrange("(q a) k -> q a k", a=2))
+        b1raw = keep.tile([P, 4], BF16)
+        nc.scalar.dma_start(out=b1raw[:], in_=be1.rearrange("(p t) -> p t", t=4))
+        b2raw = keep.tile([P, 2], BF16)
+        nc.scalar.dma_start(out=b2raw[:], in_=be2.rearrange("(q a) -> q a", a=2))
+
+        ident = keep.tile([P, P], F32)
+        make_identity(nc, ident[:])
+
+        p3c = keep.tile([P, 2, NT, 4], BF16)
+        p1 = keep.tile([P, NT, 8], BF16)
+        p2d = keep.tile([P, NT, 8, 2], BF16)
+        nc.vector.memset(p3c[:], 1.0)
+        nc.vector.memset(p1[:], 1.0)
+        nc.vector.memset(p2d[:], 1.0)
+        nc.vector.tensor_copy(out=p3c[:, 0, :, :], in_=o3_sb[:, :, 0:4])
+        nc.vector.tensor_copy(out=p3c[:, 1, :, 0:3], in_=o3_sb[:, :, 4:7])
+        vts = {}
+        planes = []
+        for kh in range(2):
+            plane = out[SCR0 + 64 * kh : SCR0 + 64 * (kh + 1), :].rearrange("r m -> (r m)")
+            planes.append(plane)
+            nc.sync.dma_start(
+                out=plane.rearrange("(c p w) -> p c w", p=P, w=8),
+                in_=p3c[:, kh, :, :].rearrange("p n t -> p (n t)").bitcast(F32).rearrange("p (c w) -> p c w", w=8),
+            )
+        for c0, c1 in V_GROUPS:
+            vt = keep.tile([P, (c1 - c0) * CH * 4], BF16, name="vt%d" % c0)
+            for kh in range(2):
+                nc.sync.dma_start(
+                    out=vt[:].bitcast(F32)[kh:P:2, :],
+                    in_=planes[kh][c0 * 1024 : c1 * 1024].partition_broadcast(64),
+                )
+            for c in range(c0, c1):
+                vts[c] = vt[:, (c - c0) * 2048 : (c - c0 + 1) * 2048]
+
+        nc.vector.tensor_copy(out=p1[:, :, 0:7], in_=o1_sb[:])
+        nc.vector.tensor_copy(
+            out=p2d[:, :, 0:7, :], in_=o2_sb[:].unsqueeze(3).to_broadcast([P, NT, D, 2])
+        )
+
+        x = keep.tile([P, NT, P], F32)
+
+        def a1(eng, g):
+            n0, n1 = 8 * g, 8 * g + 8
+            eng.tensor_tensor(
+                out=x[:, n0:n1, :].rearrange("p n (i x) -> p n i x", x=16),
+                in0=p1[:, n0:n1, :].unsqueeze(3).to_broadcast([P, 8, 8, 16]),
+                in1=p2d[:, n0:n1, :, :].rearrange("p n j k -> p n (j k)").unsqueeze(2).to_broadcast([P, 8, 8, 16]),
+                op=ALU.mult,
+            )
+
+        for g in G_GROUPS:
+            a1(nc.gpsimd, g)
+        a1(nc.vector, 0)
+        a1(nc.vector, 1)
+
+        def weight_transposes(w_sb, n_a, name):
+            grouped = keep.tile([P, n_a * P * 4], BF16, align_bytes=64, name=name + "_g")
+            g_w = grouped[:].bitcast(F32).rearrange("p (a q u) -> p a q u", a=n_a, u=2)
+            for ap in range(n_a // 2):
+                wt = psum.tile([P, 2, 2, P], F32, tag="otr", bufs=2, name=name + "_t")
+                for a2 in range(2):
+                    words = w_sb[:, 2 * ap + a2, :].bitcast(F32).rearrange("q (p u) -> q p u", u=2)
+                    for u in range(2):
+                        nc.tensor.transpose(wt[:, a2, u, :], words[:, :, u], ident[:])
+                nc.scalar.copy(
+                    out=g_w[:, 2 * ap : 2 * ap + 2, :, :],
+                    in_=wt[:].rearrange("p a u q -> p a q u"),
+                )
+            return grouped
+
+        def weight_quantise(grouped, n_a, name):
+            codes = keep.tile([P, n_a * P], U32, align_bytes=64, name=name + "_c")
+            scales = keep.tile([P, n_a * P], U8, align_bytes=64, name=name + "_s")
+            nc.vector.quantize_mx(out=codes[:].bitcast(FP8X4), scales=scales[:], in_=grouped[:])
+            return codes, scales
+
+        w1g = weight_transposes(w1_sb, 4, "w1")
+        w2g = weight_transposes(w2_sb, 2, "w2")
+        b1 = keep.tile([P, 4], F32)
+        nc.vector.tensor_copy(out=b1[:], in_=b1raw[:])
+        b2 = keep.tile([P, 2], F32)
+        nc.vector.tensor_copy(out=b2[:], in_=b2raw[:])
+        w1c, w1s = weight_quantise(w1g, 4, "w1")
+        a1(nc.vector, 2)
+        w2c, w2s = weight_quantise(w2g, 2, "w2")
+        a1(nc.vector, 3)
+
+        st = {}
+
+        def relu_exit(on_vector, dst, src, bias):
+            if on_vector:
+                nc.vector.tensor_scalar(out=dst, in0=src, scalar1=bias, scalar2=0.0, op0=ALU.add, op1=ALU.max)
+            else:
+                nc.scalar.activation(out=dst, in_=src, func=ACT.Relu, bias=bias, scale=1.0)
+
+        def copy_exit(on_vector, dst, src):
+            if on_vector:
+                nc.vector.tensor_copy(out=dst, in_=src)
+            else:
+                nc.scalar.copy(out=dst, in_=src)
+
+        def ut(c):
+            u_ps = psum.tile([P, 4, P], F32, tag="u", bufs=1)
+            for n in range(4):
+                nc.tensor.transpose(u_ps[:, n, :], x[:, 4 * c + n, :], ident[:])
+            st[("u", c)] = u_ps
+
+        def a2(c):
+            u_ps = st[("u", c)]
+            fg = work.tile([P, CH, 4], BF16, align_bytes=64)
+            nc.vector.tensor_tensor(
+                out=fg[:].rearrange("p (b n) t -> p b n t", n=4),
+                in0=u_ps[:].rearrange("p n b -> p b n").unsqueeze(3).to_broadcast([P, P, 4, 4]),
+                in1=vts[c].rearrange("p (b n t) -> p b n t", n=4, t=4),
+                op=ALU.mult,
+            )
+            st[("fg", c)] = fg
+
+        def quantise(key_in, key_out, c):
+            src = st[(key_in, c)]
+            codes = work.tile([P, CH], U32, align_bytes=64, name=key_out + "c")
+            scales = work.tile([P, CH], U8, align_bytes=64, name=key_out + "s")
+            nc.vector.quantize_mx(
+                out=codes[:].bitcast(FP8X4), scales=scales[:], in_=src[:].rearrange("p c t -> p (c t)")
+            )
+            st[(key_out, c)] = (codes, scales)
+
+        def l1(c, t):
+            fc, fs = st[("f", c)]
+            hp = psum.tile([P, CH], F32, tag="hp", bufs=3)
+            nc.tensor.matmul_mx(
+                out=hp[:],
+                lhsT=w1c[:, t * P : (t + 1) * P].bitcast(FP8X4),
+                lhsT_scale=w1s[:, t * P : (t + 1) * P],
+                rhs=fc[:].bitcast(FP8X4),
+                rhs_scale=fs[:],
+                start=True,
+                stop=True,
+            )
+            st[("hp", c, t)] = hp
+
+        def c1(c, t):
+            if t == 0:
+                h_new = work.tile([P, 4, CH], BF16, name="h")
+                st[("h", c)] = h_new
+            h = st[("h", c)]
+            relu_exit(c >= TAIL and t % 2 == 1, h[:, t, :], st[("hp", c, t)][:], b1[:, t : t + 1])
+
+        def c2(c):
+            h = st[("h", c)]
+            hg = work.tile([P, CH, 4], BF16, align_bytes=64)
+            nc.vector.tensor_copy(
+                out=hg[:].rearrange("p (c i) t -> p c t i", i=4),
+                in_=h[:].rearrange("p t (c i) -> p c t i", i=4),
+            )
+            st[("hg", c)] = hg
+
+        def l2(c):
+            hc, hs = st[("hq", c)]
+            for a in range(2):
+                o2p = psum.tile([P, CH], F32, tag="o2", bufs=2)
+                nc.tensor.matmul_mx(
+                    out=o2p[:],
+                    lhsT=w2c[:, a * P : (a + 1) * P].bitcast(FP8X4),
+                    lhsT_scale=w2s[:, a * P : (a + 1) * P],
+                    rhs=hc[:].bitcast(FP8X4),
+                    rhs_scale=hs[:],
+                    start=True,
+                    stop=True,
+                )
+                st[("o2", c, a)] = o2p
+
+        def e1(c):
+            ot = work.tile([P, 2, CH], F32)
+            for a in range(2):
+                relu_exit(c >= TAIL - 2 and a == 1, ot[:, a, :], st[("o2", c, a)][:], b2[:, a : a + 1])
+            st[("ot", c)] = ot
+
+        def et(c):
+            ot = st[("ot", c)]
+            for sp in range(2):
+                otr = psum.tile([P, 2, 2, P], F32, tag="otr", bufs=2)
+                for s2 in range(2):
+                    s = 2 * sp + s2
+                    for a in range(2):
+                        nc.tensor.transpose(otr[:, s2, a, :], ot[:, a, s * P : (s + 1) * P], ident[:])
+                st[("otr", c, sp)] = otr
+
+        def e2(c):
+            o_sb = work.tile([P, 4, M], F32, bufs=3)
+            for sp in range(2):
+                copy_exit(
+                    c >= TAIL - 3 and sp == 1,
+                    o_sb[:, 2 * sp : 2 * sp + 2, :].rearrange("p s (q a) -> p s q a", a=2),
+                    st[("otr", c, sp)][:].rearrange("p s a q -> p s q a"),
+                )
+            nc.sync.dma_start(
+                out=out[c * CH : (c + 1) * CH, :].rearrange("(s r) m -> r s m", r=P), in_=o_sb[:]
+            )
+
+        def live(c):
+            return 0 <= c < NCH
+
+        ut(0)
+        for i in range(NCH + 5):
+            if live(i - 1):
+                c1(i - 1, 0)
+                l1(i - 1, 3)
+            if live(i - 4):
+                et(i - 4)
+            if live(i):
+                a2(i)
+            if live(i - 1):
+                for t in range(1, 4):
+                    c1(i - 1, t)
+            if live(i + 1):
+                ut(i + 1)
+            if live(i - 2):
+                quantise("hg", "hq", i - 2)
+                l2(i - 2)
+            if live(i):
+                quantise("fg", "f", i)
+                for t in range(3):
+                    l1(i, t)
+            if live(i - 3):
+                e1(i - 3)
+            if live(i - 4):
+                e2(i - 4)
+            if live(i - 1):
+                c2(i - 1)

@@ -24,8 +24,10 @@ NT = B // P
 FLOPS = 2 * B * 512 * F + 2 * B * F * M
 SCR0 = B - 128
 G_GROUPS = [4, 5, 6, 7]
-TAIL = 15
-V_GROUPS = [(0, 1), (1, 2), (2, 4), (4, 8), (8, 12), (12, 16)]
+TAIL_X = 14
+TAIL_D = 2
+V_GROUPS = [(0, 1), (1, 2), (2, 4), (4, 8), (8, 12)]
+V_LATE = (12, 16)
 
 
 def tile_tensor_fusion_pa_t_kernel(tc, o1, o2, o3, We1, be1, We2, be2, out):
@@ -39,7 +41,8 @@ def tile_tensor_fusion_pa_t_kernel(tc, o1, o2, o3, We1, be1, We2, be2, out):
         o3_sb = keep.tile([P, NT, D], BF16)
         o1_sb = keep.tile([P, NT, D], BF16)
         o2_sb = keep.tile([P, NT, D], BF16)
-        for sb, dr in ((o3_sb, o3), (o1_sb, o1), (o2_sb, o2)):
+        nc.sync.dma_start(out=o3_sb[:].rearrange("p n k -> p (n k)"), in_=o3.rearrange("(p n) k -> p (n k)", p=P))
+        for sb, dr in ((o1_sb, o1), (o2_sb, o2)):
             nc.sync.dma_start(
                 out=sb[:].rearrange("p (c n) k -> p c (n k)", n=4),
                 in_=dr.rearrange("(c p n) k -> p c (n k)", p=P, n=4),
@@ -70,10 +73,11 @@ def tile_tensor_fusion_pa_t_kernel(tc, o1, o2, o3, We1, be1, We2, be2, out):
             plane = out[SCR0 + 64 * kh : SCR0 + 64 * (kh + 1), :].rearrange("r m -> (r m)")
             planes.append(plane)
             nc.sync.dma_start(
-                out=plane.rearrange("(c p w) -> p c w", p=P, w=8),
-                in_=p3c[:, kh, :, :].rearrange("p n t -> p (n t)").bitcast(F32).rearrange("p (c w) -> p c w", w=8),
+                out=plane.rearrange("(p w) -> p w", p=P),
+                in_=p3c[:, kh, :, :].rearrange("p n t -> p (n t)").bitcast(F32),
             )
-        for c0, c1 in V_GROUPS:
+
+        def v_load(c0, c1):
             vt = keep.tile([P, (c1 - c0) * CH * 4], BF16, name="vt%d" % c0)
             for kh in range(2):
                 nc.sync.dma_start(
@@ -82,6 +86,9 @@ def tile_tensor_fusion_pa_t_kernel(tc, o1, o2, o3, We1, be1, We2, be2, out):
                 )
             for c in range(c0, c1):
                 vts[c] = vt[:, (c - c0) * 2048 : (c - c0 + 1) * 2048]
+
+        for c0, c1 in V_GROUPS:
+            v_load(c0, c1)
 
         nc.vector.tensor_copy(out=p1[:, :, 0:7], in_=o1_sb[:])
         nc.vector.tensor_copy(
@@ -195,15 +202,25 @@ def tile_tensor_fusion_pa_t_kernel(tc, o1, o2, o3, We1, be1, We2, be2, out):
                 h_new = work.tile([P, 4, CH], BF16, name="h")
                 st[("h", c)] = h_new
             h = st[("h", c)]
-            relu_exit(c >= TAIL and t % 2 == 1, h[:, t, :], st[("hp", c, t)][:], b1[:, t : t + 1])
+            relu_exit(False, h[:, t, :], st[("hp", c, t)][:], b1[:, t : t + 1])
 
         def c2(c):
             h = st[("h", c)]
-            hg = work.tile([P, CH, 4], BF16, align_bytes=64)
-            nc.vector.tensor_copy(
-                out=hg[:].rearrange("p (c i) t -> p c t i", i=4),
-                in_=h[:].rearrange("p t (c i) -> p c t i", i=4),
-            )
+            hg = work.tile([P, CH, 4], BF16, align_bytes=64, bufs=1)
+            if c >= NCH - TAIL_D:
+                nc.vector.tensor_copy(
+                    out=hg[:].rearrange("p (c i) t -> p c t i", i=4),
+                    in_=h[:].rearrange("p t (c i) -> p c t i", i=4),
+                )
+            else:
+                nc.gpsimd.tensor_scalar(
+                    out=hg[:],
+                    in0=h[:].rearrange("p t c -> p c t"),
+                    scalar1=1.0,
+                    scalar2=0.0,
+                    op0=ALU.mult,
+                    op1=ALU.add,
+                )
             st[("hg", c)] = hg
 
         def l2(c):
@@ -224,7 +241,7 @@ def tile_tensor_fusion_pa_t_kernel(tc, o1, o2, o3, We1, be1, We2, be2, out):
         def e1(c):
             ot = work.tile([P, 2, CH], F32)
             for a in range(2):
-                relu_exit(c >= TAIL - 2 and a == 1, ot[:, a, :], st[("o2", c, a)][:], b2[:, a : a + 1])
+                relu_exit(c >= TAIL_X and a == 1, ot[:, a, :], st[("o2", c, a)][:], b2[:, a : a + 1])
             st[("ot", c)] = ot
 
         def et(c):
@@ -241,7 +258,7 @@ def tile_tensor_fusion_pa_t_kernel(tc, o1, o2, o3, We1, be1, We2, be2, out):
             o_sb = work.tile([P, 4, M], F32, bufs=3)
             for sp in range(2):
                 copy_exit(
-                    c >= TAIL - 3 and sp == 1,
+                    sp == 1,
                     o_sb[:, 2 * sp : 2 * sp + 2, :].rearrange("p s (q a) -> p s q a", a=2),
                     st[("otr", c, sp)][:].rearrange("p s a q -> p s q a"),
                 )
@@ -253,29 +270,40 @@ def tile_tensor_fusion_pa_t_kernel(tc, o1, o2, o3, We1, be1, We2, be2, out):
             return 0 <= c < NCH
 
         ut(0)
-        for i in range(NCH + 5):
-            if live(i - 1):
-                c1(i - 1, 0)
-                l1(i - 1, 3)
-            if live(i - 4):
-                et(i - 4)
-            if live(i):
-                a2(i)
-            if live(i - 1):
+        for k in range(NCH + 5):
+            if live(k - 1):
+                l1(k - 1, 3)
+            if k >= NCH:
+                if live(k - 3):
+                    l2(k - 3)
+                if live(k - 4):
+                    et(k - 4)
+            else:
+                if live(k - 4):
+                    et(k - 4)
+                if live(k - 3):
+                    l2(k - 3)
+            if live(k):
+                a2(k)
+            if live(k + 1):
+                ut(k + 1)
+            if live(k - 1):
                 for t in range(1, 4):
-                    c1(i - 1, t)
-            if live(i + 1):
-                ut(i + 1)
-            if live(i - 2):
-                quantise("hg", "hq", i - 2)
-                l2(i - 2)
-            if live(i):
-                quantise("fg", "f", i)
+                    c1(k - 1, t)
+            if live(k):
+                quantise("fg", "f", k)
+            if live(k - 2):
+                quantise("hg", "hq", k - 2)
+            if live(k):
                 for t in range(3):
-                    l1(i, t)
-            if live(i - 3):
-                e1(i - 3)
-            if live(i - 4):
-                e2(i - 4)
-            if live(i - 1):
-                c2(i - 1)
+                    l1(k, t)
+            if live(k - 1):
+                c2(k - 1)
+            if live(k - 3):
+                e1(k - 3)
+            if live(k - 4):
+                e2(k - 4)
+                if k - 4 == 1:
+                    v_load(V_LATE[0], V_LATE[1])
+            if live(k):
+                c1(k, 0)

@@ -26,8 +26,8 @@ SCR0 = B - 128
 G_GROUPS = [4, 5, 6, 7]
 TAIL_X = 14
 TAIL_D = 2
-V_GROUPS = [(0, 1), (1, 2), (2, 4), (4, 8), (8, 12)]
-V_LATE = (12, 16)
+V_GROUPS = [(0, 1), (1, 2), (2, 4), (4, 8), (8, 12), (12, 16)]
+OUT_BUFS = 10
 
 
 def tile_tensor_fusion_pa_t_kernel(tc, o1, o2, o3, We1, be1, We2, be2, out):
@@ -255,7 +255,7 @@ def tile_tensor_fusion_pa_t_kernel(tc, o1, o2, o3, We1, be1, We2, be2, out):
                 st[("otr", c, sp)] = otr
 
         def e2(c):
-            o_sb = work.tile([P, 4, M], F32, bufs=3)
+            o_sb = work.tile([P, 4, M], F32, bufs=OUT_BUFS)
             for sp in range(2):
                 copy_exit(
                     sp == 1,
@@ -303,7 +303,5 @@ def tile_tensor_fusion_pa_t_kernel(tc, o1, o2, o3, We1, be1, We2, be2, out):
                 e1(k - 3)
             if live(k - 4):
                 e2(k - 4)
-                if k - 4 == 1:
-                    v_load(V_LATE[0], V_LATE[1])
             if live(k):
                 c1(k, 0)

@@ -27,7 +27,7 @@ G_GROUPS = [4, 5, 6, 7]
 TAIL_X = 14
 TAIL_D = 2
 V_GROUPS = [(0, 1), (1, 2), (2, 4), (4, 8), (8, 12), (12, 16)]
-OUT_BUFS = 10
+OUT_BUFS = 4
 
 
 def tile_tensor_fusion_pa_t_kernel(tc, o1, o2, o3, We1, be1, We2, be2, out):
@@ -254,54 +254,51 @@ def tile_tensor_fusion_pa_t_kernel(tc, o1, o2, o3, We1, be1, We2, be2, out):
                         nc.tensor.transpose(otr[:, s2, a, :], ot[:, a, s * P : (s + 1) * P], ident[:])
                 st[("otr", c, sp)] = otr
 
-        def e2(c):
-            o_sb = work.tile([P, 4, M], F32, bufs=OUT_BUFS)
-            for sp in range(2):
-                copy_exit(
-                    sp == 1,
-                    o_sb[:, 2 * sp : 2 * sp + 2, :].rearrange("p s (q a) -> p s q a", a=2),
-                    st[("otr", c, sp)][:].rearrange("p s a q -> p s q a"),
-                )
-            nc.sync.dma_start(
-                out=out[c * CH : (c + 1) * CH, :].rearrange("(s r) m -> r s m", r=P), in_=o_sb[:]
+        def e2(c, sp):
+            if sp == 0:
+                o_new = work.tile([P, 4, M], F32, bufs=OUT_BUFS, name="o_sb")
+                st[("o", c)] = o_new
+            o_sb = st[("o", c)]
+            copy_exit(
+                sp == 1,
+                o_sb[:, 2 * sp : 2 * sp + 2, :].rearrange("p s (q a) -> p s q a", a=2),
+                st[("otr", c, sp)][:].rearrange("p s a q -> p s q a"),
             )
+            if sp == 1:
+                nc.sync.dma_start(
+                    out=out[c * CH : (c + 1) * CH, :].rearrange("(s r) m -> r s m", r=P), in_=o_sb[:]
+                )
 
         def live(c):
             return 0 <= c < NCH
 
         ut(0)
         for k in range(NCH + 5):
-            if live(k - 1):
-                l1(k - 1, 3)
-            if k >= NCH:
-                if live(k - 3):
-                    l2(k - 3)
-                if live(k - 4):
-                    et(k - 4)
-            else:
-                if live(k - 4):
-                    et(k - 4)
-                if live(k - 3):
-                    l2(k - 3)
             if live(k):
                 a2(k)
             if live(k + 1):
                 ut(k + 1)
-            if live(k - 1):
-                for t in range(1, 4):
-                    c1(k - 1, t)
             if live(k):
                 quantise("fg", "f", k)
             if live(k - 2):
                 quantise("hg", "hq", k - 2)
+            if live(k - 4):
+                e2(k - 4, 1)
             if live(k):
                 for t in range(3):
                     l1(k, t)
+                c1(k, 0)
+                l1(k, 3)
+            if live(k - 2):
+                l2(k - 2)
+            if live(k - 3):
+                et(k - 3)
+            if live(k):
+                for t in range(1, 4):
+                    c1(k, t)
             if live(k - 1):
                 c2(k - 1)
+            if live(k - 2):
+                e1(k - 2)
             if live(k - 3):
-                e1(k - 3)
-            if live(k - 4):
-                e2(k - 4)
-            if live(k):
-                c1(k, 0)
+                e2(k - 3, 0)

@@ -264,10 +264,10 @@ def tile_tensor_fusion_pa_t_kernel(tc, o1, o2, o3, We1, be1, We2, be2, out):
                 o_sb[:, 2 * sp : 2 * sp + 2, :].rearrange("p s (q a) -> p s q a", a=2),
                 st[("otr", c, sp)][:].rearrange("p s a q -> p s q a"),
             )
-            if sp == 1:
-                nc.sync.dma_start(
-                    out=out[c * CH : (c + 1) * CH, :].rearrange("(s r) m -> r s m", r=P), in_=o_sb[:]
-                )
+            r0 = c * CH + 2 * sp * P
+            nc.sync.dma_start(
+                out=out[r0 : r0 + 2 * P, :].rearrange("(s r) m -> r s m", r=P), in_=o_sb[:, 2 * sp : 2 * sp + 2, :]
+            )
 
         def live(c):
             return 0 <= c < NCH
@@ -278,10 +278,12 @@ def tile_tensor_fusion_pa_t_kernel(tc, o1, o2, o3, We1, be1, We2, be2, out):
                 a2(k)
             if live(k + 1):
                 ut(k + 1)
-            if live(k):
-                quantise("fg", "f", k)
             if live(k - 2):
                 quantise("hg", "hq", k - 2)
+            if live(k):
+                quantise("fg", "f", k)
+            if live(k - 1):
+                c2(k - 1)
             if live(k - 4):
                 e2(k - 4, 1)
             if live(k):
@@ -296,8 +298,6 @@ def tile_tensor_fusion_pa_t_kernel(tc, o1, o2, o3, We1, be1, We2, be2, out):
             if live(k):
                 for t in range(1, 4):
                     c1(k, t)
-            if live(k - 1):
-                c2(k - 1)
             if live(k - 2):
                 e1(k - 2)
             if live(k - 3):

@@ -59,14 +59,20 @@ def tile_tensor_fusion_pa_t_kernel(tc, o1, o2, o3, We1, be1, We2, be2, out):
         ident = keep.tile([P, P], F32)
         make_identity(nc, ident[:])
 
-        p3c = keep.tile([P, 2, NT, 4], BF16)
+        p3c = keep.tile([P, 2, 4, NT // 4, 4], BF16)
         p1 = keep.tile([P, NT, 8], BF16)
         p2d = keep.tile([P, NT, 8, 2], BF16)
         nc.vector.memset(p3c[:], 1.0)
         nc.vector.memset(p1[:], 1.0)
         nc.vector.memset(p2d[:], 1.0)
-        nc.vector.tensor_copy(out=p3c[:, 0, :, :], in_=o3_sb[:, :, 0:4])
-        nc.vector.tensor_copy(out=p3c[:, 1, :, 0:3], in_=o3_sb[:, :, 4:7])
+        nc.vector.tensor_copy(
+            out=p3c[:, 0, :, :, :].rearrange("p n q t -> p q n t"),
+            in_=o3_sb[:, :, 0:4].rearrange("p (q n) k -> p q n k", n=4),
+        )
+        nc.vector.tensor_copy(
+            out=p3c[:, 1, :, :, 0:3].rearrange("p n q t -> p q n t"),
+            in_=o3_sb[:, :, 4:7].rearrange("p (q n) k -> p q n k", n=4),
+        )
         vts = {}
         planes = []
         for kh in range(2):
@@ -74,7 +80,7 @@ def tile_tensor_fusion_pa_t_kernel(tc, o1, o2, o3, We1, be1, We2, be2, out):
             planes.append(plane)
             nc.sync.dma_start(
                 out=plane.rearrange("(p w) -> p w", p=P),
-                in_=p3c[:, kh, :, :].rearrange("p n t -> p (n t)").bitcast(F32),
+                in_=p3c[:, kh, :, :, :].rearrange("p n q t -> p (n q t)").bitcast(F32),
             )
 
         def v_load(c0, c1):
@@ -167,9 +173,9 @@ def tile_tensor_fusion_pa_t_kernel(tc, o1, o2, o3, We1, be1, We2, be2, out):
             u_ps = st[("u", c)]
             fg = work.tile([P, CH, 4], BF16, align_bytes=64)
             nc.vector.tensor_tensor(
-                out=fg[:].rearrange("p (b n) t -> p b n t", n=4),
-                in0=u_ps[:].rearrange("p n b -> p b n").unsqueeze(3).to_broadcast([P, P, 4, 4]),
-                in1=vts[c].rearrange("p (b n t) -> p b n t", n=4, t=4),
+                out=fg[:].rearrange("p (n r q) t -> p n r q t", n=4, r=8),
+                in0=u_ps[:].rearrange("p n (r q) -> p n r q", r=8).unsqueeze(4).to_broadcast([P, 4, 8, 16, 4]),
+                in1=vts[c].rearrange("p (r n q t) -> p n r q t", r=8, n=4, t=4),
                 op=ALU.mult,
             )
             st[("fg", c)] = fg
@@ -264,9 +270,9 @@ def tile_tensor_fusion_pa_t_kernel(tc, o1, o2, o3, We1, be1, We2, be2, out):
                 o_sb[:, 2 * sp : 2 * sp + 2, :].rearrange("p s (q a) -> p s q a", a=2),
                 st[("otr", c, sp)][:].rearrange("p s a q -> p s q a"),
             )
-            r0 = c * CH + 2 * sp * P
             nc.sync.dma_start(
-                out=out[r0 : r0 + 2 * P, :].rearrange("(s r) m -> r s m", r=P), in_=o_sb[:, 2 * sp : 2 * sp + 2, :]
+                out=out[c * CH : (c + 1) * CH, :].rearrange("(r s) m -> r s m", s=4)[:, 2 * sp : 2 * sp + 2, :],
+                in_=o_sb[:, 2 * sp : 2 * sp + 2, :],
             )
 
         def live(c):

@@ -23,7 +23,7 @@ NCH = B // CH
 NT = B // P
 FLOPS = 2 * B * 512 * F + 2 * B * F * M
 SCR0 = B - 128
-G_GROUPS = [4, 5, 6, 7]
+S_LATE = {0: 3, 1: 4, 2: 5}
 TAIL_X = 14
 TAIL_D = 2
 V_GROUPS = [(0, 1), (1, 2), (2, 4), (4, 8), (8, 12), (12, 16)]
@@ -56,15 +56,15 @@ def tile_tensor_fusion_pa_t_kernel(tc, o1, o2, o3, We1, be1, We2, be2, out):
         b2raw = keep.tile([P, 2], BF16)
         nc.scalar.dma_start(out=b2raw[:], in_=be2.rearrange("(q a) -> q a", a=2))
 
+        p3c = keep.tile([P, 2, 4, NT // 4, 4], BF16)
+        p1 = keep.tile([P, NT, 8], BF16)
+        p2 = keep.tile([P, NT, 8], BF16)
+        nc.gpsimd.memset(p3c[:], 1.0)
+        nc.gpsimd.memset(p1[:], 1.0)
+        nc.gpsimd.memset(p2[:], 1.0)
         ident = keep.tile([P, P], F32)
         make_identity(nc, ident[:])
 
-        p3c = keep.tile([P, 2, 4, NT // 4, 4], BF16)
-        p1 = keep.tile([P, NT, 8], BF16)
-        p2d = keep.tile([P, NT, 8, 2], BF16)
-        nc.vector.memset(p3c[:], 1.0)
-        nc.vector.memset(p1[:], 1.0)
-        nc.vector.memset(p2d[:], 1.0)
         nc.vector.tensor_copy(
             out=p3c[:, 0, :, :, :].rearrange("p n q t -> p q n t"),
             in_=o3_sb[:, :, 0:4].rearrange("p (q n) k -> p q n k", n=4),
@@ -96,41 +96,44 @@ def tile_tensor_fusion_pa_t_kernel(tc, o1, o2, o3, We1, be1, We2, be2, out):
         for c0, c1 in V_GROUPS:
             v_load(c0, c1)
 
-        nc.vector.tensor_copy(out=p1[:, :, 0:7], in_=o1_sb[:])
-        nc.vector.tensor_copy(
-            out=p2d[:, :, 0:7, :], in_=o2_sb[:].unsqueeze(3).to_broadcast([P, NT, D, 2])
-        )
+        nc.scalar.copy(out=p1[:, :, 0:7], in_=o1_sb[:])
+        nc.scalar.copy(out=p2[:, :, 0:7], in_=o2_sb[:])
 
+        x_nd = keep.tile([P, NT, 64], F32)
         x = keep.tile([P, NT, P], F32)
 
-        def a1(eng, g):
-            n0, n1 = 8 * g, 8 * g + 8
-            eng.tensor_tensor(
-                out=x[:, n0:n1, :].rearrange("p n (i x) -> p n i x", x=16),
-                in0=p1[:, n0:n1, :].unsqueeze(3).to_broadcast([P, 8, 8, 16]),
-                in1=p2d[:, n0:n1, :, :].rearrange("p n j k -> p n (j k)").unsqueeze(2).to_broadcast([P, 8, 8, 16]),
+        def a1(n0, n1):
+            nc.vector.tensor_tensor(
+                out=x_nd[:, n0:n1, :].rearrange("p n (i j) -> p n i j", j=8),
+                in0=p1[:, n0:n1, :].unsqueeze(3).to_broadcast([P, n1 - n0, 8, 8]),
+                in1=p2[:, n0:n1, :].unsqueeze(2).to_broadcast([P, n1 - n0, 8, 8]),
                 op=ALU.mult,
             )
 
-        for g in G_GROUPS:
-            a1(nc.gpsimd, g)
-        a1(nc.vector, 0)
-        a1(nc.vector, 1)
+        def dup(on_gpsimd, g):
+            n0, n1 = 8 * g, 8 * g + 8
+            dst = x[:, n0:n1, :].rearrange("p n (m d) -> p n m d", d=2)
+            src = x_nd[:, n0:n1, :].unsqueeze(3).to_broadcast([P, 8, 64, 2])
+            if on_gpsimd:
+                nc.gpsimd.tensor_scalar(out=dst, in0=src, scalar1=1.0, scalar2=0.0, op0=ALU.mult, op1=ALU.add)
+            else:
+                nc.scalar.copy(out=dst, in_=src)
 
-        def weight_transposes(w_sb, n_a, name):
+        def weight_tile(n_a, name):
             grouped = keep.tile([P, n_a * P * 4], BF16, align_bytes=64, name=name + "_g")
-            g_w = grouped[:].bitcast(F32).rearrange("p (a q u) -> p a q u", a=n_a, u=2)
-            for ap in range(n_a // 2):
-                wt = psum.tile([P, 2, 2, P], F32, tag="otr", bufs=2, name=name + "_t")
-                for a2 in range(2):
-                    words = w_sb[:, 2 * ap + a2, :].bitcast(F32).rearrange("q (p u) -> q p u", u=2)
-                    for u in range(2):
-                        nc.tensor.transpose(wt[:, a2, u, :], words[:, :, u], ident[:])
-                nc.scalar.copy(
-                    out=g_w[:, 2 * ap : 2 * ap + 2, :, :],
-                    in_=wt[:].rearrange("p a u q -> p a q u"),
-                )
             return grouped
+
+        def weight_pair(w_sb, grouped, n_a, ap, name):
+            g_w = grouped[:].bitcast(F32).rearrange("p (a q u) -> p a q u", a=n_a, u=2)
+            wt = psum.tile([P, 2, 2, P], F32, tag="otr", bufs=2, name=name + "_t")
+            for a2 in range(2):
+                words = w_sb[:, 2 * ap + a2, :].bitcast(F32).rearrange("q (p u) -> q p u", u=2)
+                for u in range(2):
+                    nc.tensor.transpose(wt[:, a2, u, :], words[:, :, u], ident[:])
+            nc.scalar.copy(
+                out=g_w[:, 2 * ap : 2 * ap + 2, :, :],
+                in_=wt[:].rearrange("p a u q -> p a q u"),
+            )
 
         def weight_quantise(grouped, n_a, name):
             codes = keep.tile([P, n_a * P], U32, align_bytes=64, name=name + "_c")
@@ -138,18 +141,28 @@ def tile_tensor_fusion_pa_t_kernel(tc, o1, o2, o3, We1, be1, We2, be2, out):
             nc.vector.quantize_mx(out=codes[:].bitcast(FP8X4), scales=scales[:], in_=grouped[:])
             return codes, scales
 
-        w1g = weight_transposes(w1_sb, 4, "w1")
-        w2g = weight_transposes(w2_sb, 2, "w2")
+        w1g = weight_tile(4, "w1")
+        w2g = weight_tile(2, "w2")
         b1 = keep.tile([P, 4], F32)
-        nc.vector.tensor_copy(out=b1[:], in_=b1raw[:])
         b2 = keep.tile([P, 2], F32)
-        nc.vector.tensor_copy(out=b2[:], in_=b2raw[:])
+        a1(0, 16)
+        dup(False, 0)
+        weight_pair(w1_sb, w1g, 4, 0, "w1")
+        weight_pair(w1_sb, w1g, 4, 1, "w1")
+        a1(16, 32)
+        dup(False, 1)
+        weight_pair(w2_sb, w2g, 2, 0, "w2")
+        nc.scalar.copy(out=b1[:], in_=b1raw[:])
+        nc.scalar.copy(out=b2[:], in_=b2raw[:])
+        a1(32, 48)
         w1c, w1s = weight_quantise(w1g, 4, "w1")
-        a1(nc.vector, 2)
-        w2c, w2s = weight_quantise(w2g, 2, "w2")
-        a1(nc.vector, 3)
+        dup(False, 2)
+        a1(48, 64)
+        dup(True, 6)
+        dup(True, 7)
 
         st = {}
+        w2q = []
 
         def relu_exit(on_vector, dst, src, bias):
             if on_vector:
@@ -235,8 +248,8 @@ def tile_tensor_fusion_pa_t_kernel(tc, o1, o2, o3, We1, be1, We2, be2, out):
                 o2p = psum.tile([P, CH], F32, tag="o2", bufs=2)
                 nc.tensor.matmul_mx(
                     out=o2p[:],
-                    lhsT=w2c[:, a * P : (a + 1) * P].bitcast(FP8X4),
-                    lhsT_scale=w2s[:, a * P : (a + 1) * P],
+                    lhsT=w2q[0][:, a * P : (a + 1) * P].bitcast(FP8X4),
+                    lhsT_scale=w2q[1][:, a * P : (a + 1) * P],
                     rhs=hc[:].bitcast(FP8X4),
                     rhs_scale=hs[:],
                     start=True,
@@ -288,6 +301,8 @@ def tile_tensor_fusion_pa_t_kernel(tc, o1, o2, o3, We1, be1, We2, be2, out):
                 quantise("hg", "hq", k - 2)
             if live(k):
                 quantise("fg", "f", k)
+            if k == 0:
+                w2q.extend(weight_quantise(w2g, 2, "w2"))
             if live(k - 1):
                 c2(k - 1)
             if live(k - 4):
@@ -304,6 +319,8 @@ def tile_tensor_fusion_pa_t_kernel(tc, o1, o2, o3, We1, be1, We2, be2, out):
             if live(k):
                 for t in range(1, 4):
                     c1(k, t)
+            if k in S_LATE:
+                dup(False, S_LATE[k])
             if live(k - 2):
                 e1(k - 2)
             if live(k - 3):

@@ -23,7 +23,7 @@ NCH = B // CH
 NT = B // P
 FLOPS = 2 * B * 512 * F + 2 * B * F * M
 SCR0 = B - 128
-S_LATE = {0: 3, 1: 4, 2: 5}
+EARLY_CH = 4
 TAIL_X = 14
 TAIL_D = 2
 V_GROUPS = [(0, 1), (1, 2), (2, 4), (4, 8), (8, 12), (12, 16)]
@@ -42,11 +42,15 @@ def tile_tensor_fusion_pa_t_kernel(tc, o1, o2, o3, We1, be1, We2, be2, out):
         o1_sb = keep.tile([P, NT, D], BF16)
         o2_sb = keep.tile([P, NT, D], BF16)
         nc.sync.dma_start(out=o3_sb[:].rearrange("p n k -> p (n k)"), in_=o3.rearrange("(p n) k -> p (n k)", p=P))
-        for sb, dr in ((o1_sb, o1), (o2_sb, o2)):
-            nc.sync.dma_start(
-                out=sb[:].rearrange("p (c n) k -> p c (n k)", n=4),
-                in_=dr.rearrange("(c p n) k -> p c (n k)", p=P, n=4),
-            )
+        for c0, c1 in ((0, EARLY_CH), (EARLY_CH, NCH)):
+            for sb, dr in ((o1_sb, o1), (o2_sb, o2)):
+                nc.sync.dma_start(
+                    out=sb[:, 4 * c0 : 4 * c1, :].rearrange("p (c n) k -> p c (n k)", n=4),
+                    in_=dr[c0 * CH : c1 * CH, :].rearrange("(c p n) k -> p c (n k)", p=P, n=4),
+                )
+        warm = keep.tile([P, 2], F32)
+        nc.vector.memset(warm[:], 0.0)
+        nc.scalar.activation(out=warm[:, 1:2], in_=warm[:, 0:1], func=ACT.Relu)
         w1_sb = keep.tile([P, 4, 512], BF16)
         nc.scalar.dma_start(out=w1_sb[:], in_=We1.rearrange("(q a) k -> q a k", a=4))
         w2_sb = keep.tile([P, 2, 512], BF16)
@@ -96,8 +100,9 @@ def tile_tensor_fusion_pa_t_kernel(tc, o1, o2, o3, We1, be1, We2, be2, out):
         for c0, c1 in V_GROUPS:
             v_load(c0, c1)
 
-        nc.scalar.copy(out=p1[:, :, 0:7], in_=o1_sb[:])
-        nc.scalar.copy(out=p2[:, :, 0:7], in_=o2_sb[:])
+        for n0, n1 in ((0, 4 * EARLY_CH), (4 * EARLY_CH, NT)):
+            nc.scalar.copy(out=p1[:, n0:n1, 0:7], in_=o1_sb[:, n0:n1, :])
+            nc.scalar.copy(out=p2[:, n0:n1, 0:7], in_=o2_sb[:, n0:n1, :])
 
         x_nd = keep.tile([P, NT, 64], F32)
         x = keep.tile([P, NT, P], F32)
@@ -157,9 +162,11 @@ def tile_tensor_fusion_pa_t_kernel(tc, o1, o2, o3, We1, be1, We2, be2, out):
         a1(32, 48)
         w1c, w1s = weight_quantise(w1g, 4, "w1")
         dup(False, 2)
-        a1(48, 64)
+        dup(False, 3)
+        dup(False, 4)
+        a1(48, 56)
         dup(True, 6)
-        dup(True, 7)
+        dup(True, 5)
 
         st = {}
         w2q = []
@@ -303,6 +310,8 @@ def tile_tensor_fusion_pa_t_kernel(tc, o1, o2, o3, We1, be1, We2, be2, out):
                 quantise("fg", "f", k)
             if k == 0:
                 w2q.extend(weight_quantise(w2g, 2, "w2"))
+                a1(56, 64)
+                dup(True, 7)
             if live(k - 1):
                 c2(k - 1)
             if live(k - 4):
@@ -319,8 +328,6 @@ def tile_tensor_fusion_pa_t_kernel(tc, o1, o2, o3, We1, be1, We2, be2, out):
             if live(k):
                 for t in range(1, 4):
                     c1(k, t)
-            if k in S_LATE:
-                dup(False, S_LATE[k])
             if live(k - 2):
                 e1(k - 2)
             if live(k - 3):

@@ -170,6 +170,9 @@ def tile_tensor_fusion_pa_t_kernel(tc, o1, o2, o3, We1, be1, We2, be2, out):
 
         st = {}
         w2q = []
+        g0 = keep.tile([P, CH, 4], BF16, align_bytes=64, name="g0")
+        g1 = keep.tile([P, CH, 4], BF16, align_bytes=64, name="g1")
+        gbuf = [g0, g1]
 
         def relu_exit(on_vector, dst, src, bias):
             if on_vector:
@@ -191,7 +194,7 @@ def tile_tensor_fusion_pa_t_kernel(tc, o1, o2, o3, We1, be1, We2, be2, out):
 
         def a2(c):
             u_ps = st[("u", c)]
-            fg = work.tile([P, CH, 4], BF16, align_bytes=64)
+            fg = gbuf[c % 2]
             nc.vector.tensor_tensor(
                 out=fg[:].rearrange("p (n r q) t -> p n r q t", n=4, r=8),
                 in0=u_ps[:].rearrange("p n (r q) -> p n r q", r=8).unsqueeze(4).to_broadcast([P, 4, 8, 16, 4]),
@@ -232,7 +235,7 @@ def tile_tensor_fusion_pa_t_kernel(tc, o1, o2, o3, We1, be1, We2, be2, out):
 
         def c2(c):
             h = st[("h", c)]
-            hg = work.tile([P, CH, 4], BF16, align_bytes=64, bufs=1)
+            hg = gbuf[(c + 1) % 2]
             if c >= NCH - TAIL_D:
                 nc.vector.tensor_copy(
                     out=hg[:].rearrange("p (c i) t -> p c t i", i=4),
@@ -281,12 +284,12 @@ def tile_tensor_fusion_pa_t_kernel(tc, o1, o2, o3, We1, be1, We2, be2, out):
                 st[("otr", c, sp)] = otr
 
         def e2(c, sp):
-            if sp == 0:
+            if sp == 1:
                 o_new = work.tile([P, 4, M], F32, bufs=OUT_BUFS, name="o_sb")
                 st[("o", c)] = o_new
             o_sb = st[("o", c)]
             copy_exit(
-                sp == 1,
+                sp == 0,
                 o_sb[:, 2 * sp : 2 * sp + 2, :].rearrange("p s (q a) -> p s q a", a=2),
                 st[("otr", c, sp)][:].rearrange("p s a q -> p s q a"),
             )
@@ -304,18 +307,18 @@ def tile_tensor_fusion_pa_t_kernel(tc, o1, o2, o3, We1, be1, We2, be2, out):
                 a2(k)
             if live(k + 1):
                 ut(k + 1)
-            if live(k - 2):
-                quantise("hg", "hq", k - 2)
+            if live(k - 4):
+                e2(k - 4, 0)
             if live(k):
                 quantise("fg", "f", k)
             if k == 0:
                 w2q.extend(weight_quantise(w2g, 2, "w2"))
                 a1(56, 64)
                 dup(True, 7)
+            if live(k - 2):
+                quantise("hg", "hq", k - 2)
             if live(k - 1):
                 c2(k - 1)
-            if live(k - 4):
-                e2(k - 4, 1)
             if live(k):
                 for t in range(3):
                     l1(k, t)
@@ -331,4 +334,4 @@ def tile_tensor_fusion_pa_t_kernel(tc, o1, o2, o3, We1, be1, We2, be2, out):
             if live(k - 2):
                 e1(k - 2)
             if live(k - 3):
-                e2(k - 3, 0)
+                e2(k - 3, 1)

@@ -172,7 +172,8 @@ def tile_tensor_fusion_pa_t_kernel(tc, o1, o2, o3, We1, be1, We2, be2, out):
         w2q = []
         g0 = keep.tile([P, CH, 4], BF16, align_bytes=64, name="g0")
         g1 = keep.tile([P, CH, 4], BF16, align_bytes=64, name="g1")
-        gbuf = [g0, g1]
+        g2 = keep.tile([P, CH, 4], BF16, align_bytes=64, name="g2")
+        gbuf = [g0, g1, g2]
 
         def relu_exit(on_vector, dst, src, bias):
             if on_vector:
@@ -194,7 +195,7 @@ def tile_tensor_fusion_pa_t_kernel(tc, o1, o2, o3, We1, be1, We2, be2, out):
 
         def a2(c):
             u_ps = st[("u", c)]
-            fg = gbuf[c % 2]
+            fg = gbuf[c % 3]
             nc.vector.tensor_tensor(
                 out=fg[:].rearrange("p (n r q) t -> p n r q t", n=4, r=8),
                 in0=u_ps[:].rearrange("p n (r q) -> p n r q", r=8).unsqueeze(4).to_broadcast([P, 4, 8, 16, 4]),
@@ -228,14 +229,14 @@ def tile_tensor_fusion_pa_t_kernel(tc, o1, o2, o3, We1, be1, We2, be2, out):
 
         def c1(c, t):
             if t == 0:
-                h_new = work.tile([P, 4, CH], BF16, name="h")
+                h_new = work.tile([P, 4, CH], BF16, name="h", bufs=3)
                 st[("h", c)] = h_new
             h = st[("h", c)]
             relu_exit(False, h[:, t, :], st[("hp", c, t)][:], b1[:, t : t + 1])
 
         def c2(c):
             h = st[("h", c)]
-            hg = gbuf[(c + 1) % 2]
+            hg = gbuf[(c + 1) % 3]
             if c >= NCH - TAIL_D:
                 nc.vector.tensor_copy(
                     out=hg[:].rearrange("p (c i) t -> p c t i", i=4),
@@ -273,15 +274,14 @@ def tile_tensor_fusion_pa_t_kernel(tc, o1, o2, o3, We1, be1, We2, be2, out):
                 relu_exit(c >= TAIL_X and a == 1, ot[:, a, :], st[("o2", c, a)][:], b2[:, a : a + 1])
             st[("ot", c)] = ot
 
-        def et(c):
+        def et(c, sp):
             ot = st[("ot", c)]
-            for sp in range(2):
-                otr = psum.tile([P, 2, 2, P], F32, tag="otr", bufs=2)
-                for s2 in range(2):
-                    s = 2 * sp + s2
-                    for a in range(2):
-                        nc.tensor.transpose(otr[:, s2, a, :], ot[:, a, s * P : (s + 1) * P], ident[:])
-                st[("otr", c, sp)] = otr
+            otr = psum.tile([P, 2, 2, P], F32, tag="otr", bufs=2)
+            for s2 in range(2):
+                s = 2 * sp + s2
+                for a in range(2):
+                    nc.tensor.transpose(otr[:, s2, a, :], ot[:, a, s * P : (s + 1) * P], ident[:])
+            st[("otr", c, sp)] = otr
 
         def e2(c, sp):
             if sp == 1:
@@ -323,11 +323,14 @@ def tile_tensor_fusion_pa_t_kernel(tc, o1, o2, o3, We1, be1, We2, be2, out):
                 for t in range(3):
                     l1(k, t)
                 c1(k, 0)
+            if live(k - 3):
+                et(k - 3, 0)
+            if live(k):
                 l1(k, 3)
             if live(k - 2):
                 l2(k - 2)
             if live(k - 3):
-                et(k - 3)
+                et(k - 3, 1)
             if live(k):
                 for t in range(1, 4):
                     c1(k, t)

@@ -130,7 +130,7 @@ def tile_tensor_fusion_pa_t_kernel(tc, o1, o2, o3, We1, be1, We2, be2, out):
 
         def weight_pair(w_sb, grouped, n_a, ap, name):
             g_w = grouped[:].bitcast(F32).rearrange("p (a q u) -> p a q u", a=n_a, u=2)
-            wt = psum.tile([P, 2, 2, P], F32, tag="otr", bufs=2, name=name + "_t")
+            wt = psum.tile([P, 2, 2, P], F32, tag="r", bufs=7, name=name + "_t")
             for a2 in range(2):
                 words = w_sb[:, 2 * ap + a2, :].bitcast(F32).rearrange("q (p u) -> q p u", u=2)
                 for u in range(2):
@@ -215,7 +215,7 @@ def tile_tensor_fusion_pa_t_kernel(tc, o1, o2, o3, We1, be1, We2, be2, out):
 
         def l1(c, t):
             fc, fs = st[("f", c)]
-            hp = psum.tile([P, CH], F32, tag="hp", bufs=3)
+            hp = psum.tile([P, CH], F32, tag="r", bufs=7)
             nc.tensor.matmul_mx(
                 out=hp[:],
                 lhsT=w1c[:, t * P : (t + 1) * P].bitcast(FP8X4),
@@ -256,7 +256,7 @@ def tile_tensor_fusion_pa_t_kernel(tc, o1, o2, o3, We1, be1, We2, be2, out):
         def l2(c):
             hc, hs = st[("hq", c)]
             for a in range(2):
-                o2p = psum.tile([P, CH], F32, tag="o2", bufs=2)
+                o2p = psum.tile([P, CH], F32, tag="r", bufs=7)
                 nc.tensor.matmul_mx(
                     out=o2p[:],
                     lhsT=w2q[0][:, a * P : (a + 1) * P].bitcast(FP8X4),
@@ -276,7 +276,7 @@ def tile_tensor_fusion_pa_t_kernel(tc, o1, o2, o3, We1, be1, We2, be2, out):
 
         def et(c, sp):
             ot = st[("ot", c)]
-            otr = psum.tile([P, 2, 2, P], F32, tag="otr", bufs=2)
+            otr = psum.tile([P, 2, 2, P], F32, tag="r", bufs=7)
             for s2 in range(2):
                 s = 2 * sp + s2
                 for a in range(2):
@@ -284,7 +284,7 @@ def tile_tensor_fusion_pa_t_kernel(tc, o1, o2, o3, We1, be1, We2, be2, out):
             st[("otr", c, sp)] = otr
 
         def e2(c, sp):
-            if sp == 1:
+            if ("o", c) not in st:
                 o_new = work.tile([P, 4, M], F32, bufs=OUT_BUFS, name="o_sb")
                 st[("o", c)] = o_new
             o_sb = st[("o", c)]
@@ -307,7 +307,7 @@ def tile_tensor_fusion_pa_t_kernel(tc, o1, o2, o3, We1, be1, We2, be2, out):
                 a2(k)
             if live(k + 1):
                 ut(k + 1)
-            if live(k - 4):
+            if live(k - 4) and live(k):
                 e2(k - 4, 0)
             if live(k):
                 quantise("fg", "f", k)
@@ -315,21 +315,26 @@ def tile_tensor_fusion_pa_t_kernel(tc, o1, o2, o3, We1, be1, We2, be2, out):
                 w2q.extend(weight_quantise(w2g, 2, "w2"))
                 a1(56, 64)
                 dup(True, 7)
-            if live(k - 2):
+            if live(k - 2) and k <= NCH:
                 quantise("hg", "hq", k - 2)
             if live(k - 1):
                 c2(k - 1)
+            if live(k - 4) and not live(k):
+                e2(k - 4, 0)
+            if k == NCH:
+                quantise("hg", "hq", k - 1)
             if live(k):
                 for t in range(3):
                     l1(k, t)
                 c1(k, 0)
-            if live(k - 3):
-                et(k - 3, 0)
-            if live(k):
+                if live(k - 3):
+                    et(k - 3, 0)
                 l1(k, 3)
             if live(k - 2):
                 l2(k - 2)
             if live(k - 3):
+                if not live(k):
+                    et(k - 3, 0)
                 et(k - 3, 1)
             if live(k):
                 for t in range(1, 4):

@@ -52,13 +52,9 @@ def tile_tensor_fusion_pa_t_kernel(tc, o1, o2, o3, We1, be1, We2, be2, out):
         nc.vector.memset(warm[:], 0.0)
         nc.scalar.activation(out=warm[:, 1:2], in_=warm[:, 0:1], func=ACT.Relu)
         w1_sb = keep.tile([P, 4, 512], BF16)
-        nc.scalar.dma_start(out=w1_sb[:], in_=We1.rearrange("(q a) k -> q a k", a=4))
         w2_sb = keep.tile([P, 2, 512], BF16)
-        nc.scalar.dma_start(out=w2_sb[:], in_=We2.rearrange("(q a) k -> q a k", a=2))
         b1raw = keep.tile([P, 4], BF16)
-        nc.scalar.dma_start(out=b1raw[:], in_=be1.rearrange("(p t) -> p t", t=4))
         b2raw = keep.tile([P, 2], BF16)
-        nc.scalar.dma_start(out=b2raw[:], in_=be2.rearrange("(q a) -> q a", a=2))
 
         p3c = keep.tile([P, 2, 4, NT // 4, 4], BF16)
         p1 = keep.tile([P, NT, 8], BF16)
@@ -86,6 +82,11 @@ def tile_tensor_fusion_pa_t_kernel(tc, o1, o2, o3, We1, be1, We2, be2, out):
                 out=plane.rearrange("(p w) -> p w", p=P),
                 in_=p3c[:, kh, :, :, :].rearrange("p n q t -> p (n q t)").bitcast(F32),
             )
+
+        nc.sync.dma_start(out=w1_sb[:], in_=We1.rearrange("(q a) k -> q a k", a=4))
+        nc.sync.dma_start(out=w2_sb[:], in_=We2.rearrange("(q a) k -> q a k", a=2))
+        nc.sync.dma_start(out=b1raw[:], in_=be1.rearrange("(p t) -> p t", t=4))
+        nc.sync.dma_start(out=b2raw[:], in_=be2.rearrange("(q a) -> q a", a=2))
 
         def v_load(c0, c1):
             vt = keep.tile([P, (c1 - c0) * CH * 4], BF16, name="vt%d" % c0)
@@ -160,7 +161,6 @@ def tile_tensor_fusion_pa_t_kernel(tc, o1, o2, o3, We1, be1, We2, be2, out):
         nc.scalar.copy(out=b1[:], in_=b1raw[:])
         nc.scalar.copy(out=b2[:], in_=b2raw[:])
         a1(32, 48)
-        w1c, w1s = weight_quantise(w1g, 4, "w1")
         dup(False, 2)
         dup(False, 3)
         dup(False, 4)
@@ -170,6 +170,7 @@ def tile_tensor_fusion_pa_t_kernel(tc, o1, o2, o3, We1, be1, We2, be2, out):
 
         st = {}
         w2q = []
+        w1q = []
         g0 = keep.tile([P, CH, 4], BF16, align_bytes=64, name="g0")
         g1 = keep.tile([P, CH, 4], BF16, align_bytes=64, name="g1")
         g2 = keep.tile([P, CH, 4], BF16, align_bytes=64, name="g2")
@@ -218,8 +219,8 @@ def tile_tensor_fusion_pa_t_kernel(tc, o1, o2, o3, We1, be1, We2, be2, out):
             hp = psum.tile([P, CH], F32, tag="r", bufs=7)
             nc.tensor.matmul_mx(
                 out=hp[:],
-                lhsT=w1c[:, t * P : (t + 1) * P].bitcast(FP8X4),
-                lhsT_scale=w1s[:, t * P : (t + 1) * P],
+                lhsT=w1q[0][:, t * P : (t + 1) * P].bitcast(FP8X4),
+                lhsT_scale=w1q[1][:, t * P : (t + 1) * P],
                 rhs=fc[:].bitcast(FP8X4),
                 rhs_scale=fs[:],
                 start=True,
@@ -309,6 +310,8 @@ def tile_tensor_fusion_pa_t_kernel(tc, o1, o2, o3, We1, be1, We2, be2, out):
                 ut(k + 1)
             if live(k - 4) and live(k):
                 e2(k - 4, 0)
+            if k == 0:
+                w1q.extend(weight_quantise(w1g, 4, "w1"))
             if live(k):
                 quantise("fg", "f", k)
             if k == 0:

@@ -147,12 +147,21 @@ def tile_tensor_fusion_pa_t_kernel(tc, o1, o2, o3, We1, be1, We2, be2, out):
             nc.vector.quantize_mx(out=codes[:].bitcast(FP8X4), scales=scales[:], in_=grouped[:])
             return codes, scales
 
+        st = {}
+
+        def ut(c):
+            u_ps = psum.tile([P, 4, P], F32, tag="u", bufs=1)
+            for n in range(4):
+                nc.tensor.transpose(u_ps[:, n, :], x[:, 4 * c + n, :], ident[:])
+            st[("u", c)] = u_ps
+
         w1g = weight_tile(4, "w1")
         w2g = weight_tile(2, "w2")
         b1 = keep.tile([P, 4], F32)
         b2 = keep.tile([P, 2], F32)
         a1(0, 16)
         dup(False, 0)
+        ut(0)
         weight_pair(w1_sb, w1g, 4, 0, "w1")
         weight_pair(w1_sb, w1g, 4, 1, "w1")
         a1(16, 32)
@@ -162,13 +171,10 @@ def tile_tensor_fusion_pa_t_kernel(tc, o1, o2, o3, We1, be1, We2, be2, out):
         nc.scalar.copy(out=b2[:], in_=b2raw[:])
         a1(32, 48)
         dup(False, 2)
-        dup(False, 3)
-        dup(False, 4)
         a1(48, 56)
         dup(True, 6)
         dup(True, 5)
 
-        st = {}
         w2q = []
         w1q = []
         g0 = keep.tile([P, CH, 4], BF16, align_bytes=64, name="g0")
@@ -187,12 +193,6 @@ def tile_tensor_fusion_pa_t_kernel(tc, o1, o2, o3, We1, be1, We2, be2, out):
                 nc.vector.tensor_copy(out=dst, in_=src)
             else:
                 nc.scalar.copy(out=dst, in_=src)
-
-        def ut(c):
-            u_ps = psum.tile([P, 4, P], F32, tag="u", bufs=1)
-            for n in range(4):
-                nc.tensor.transpose(u_ps[:, n, :], x[:, 4 * c + n, :], ident[:])
-            st[("u", c)] = u_ps
 
         def a2(c):
             u_ps = st[("u", c)]
@@ -302,7 +302,6 @@ def tile_tensor_fusion_pa_t_kernel(tc, o1, o2, o3, We1, be1, We2, be2, out):
         def live(c):
             return 0 <= c < NCH
 
-        ut(0)
         for k in range(NCH + 5):
             if live(k):
                 a2(k)
@@ -346,3 +345,5 @@ def tile_tensor_fusion_pa_t_kernel(tc, o1, o2, o3, We1, be1, We2, be2, out):
                 e1(k - 2)
             if live(k - 3):
                 e2(k - 3, 1)
+            if k < 2:
+                dup(False, 3 + k)

@@ -233,7 +233,7 @@ def tile_tensor_fusion_pa_t_kernel(tc, o1, o2, o3, We1, be1, We2, be2, out):
                 h_new = work.tile([P, 4, CH], BF16, name="h", bufs=3)
                 st[("h", c)] = h_new
             h = st[("h", c)]
-            relu_exit(False, h[:, t, :], st[("hp", c, t)][:], b1[:, t : t + 1])
+            relu_exit(c == NCH - 1 and t >= 2, h[:, t, :], st[("hp", c, t)][:], b1[:, t : t + 1])
 
         def c2(c):
             h = st[("h", c)]

from contextlib import ExitStack

import concourse.bass as bass
import concourse.mybir as mybir
import concourse.tile as tile
from concourse.masks import make_identity

F32 = mybir.dt.float32
BF16 = mybir.dt.bfloat16
U32 = mybir.dt.uint32
U8 = mybir.dt.uint8
FP8X4 = mybir.dt.float8_e4m3fn_x4
ALU = mybir.AluOpType
ACT = mybir.ActivationFunctionType

P = 128
B = 8192
D = 7
F = 512
M = 256
CH = 512
NCH = B // CH
NT = B // P
FLOPS = 2 * B * 512 * F + 2 * B * F * M
SCR0 = B - 128
EARLY_CH = 4
TAIL_X = 14
TAIL_D = 2
V_GROUPS = [(0, 1), (1, 2), (2, 4), (4, 8), (8, 12), (12, 16)]
OUT_BUFS = 4


def tile_tensor_fusion_pa_t_kernel(tc, o1, o2, o3, We1, be1, We2, be2, out):
    nc = tc.nc
    with ExitStack() as ctx:
        keep = ctx.enter_context(tc.tile_pool(name="keep", bufs=1))
        work = ctx.enter_context(tc.tile_pool(name="work", bufs=2))
        psum = ctx.enter_context(tc.psum_pool(name="psum", bufs=1))
        ctx.enter_context(tc.manual_schedule())

        o3_sb = keep.tile([P, NT, D], BF16)
        o1_sb = keep.tile([P, NT, D], BF16)
        o2_sb = keep.tile([P, NT, D], BF16)
        nc.sync.dma_start(out=o3_sb[:].rearrange("p n k -> p (n k)"), in_=o3.rearrange("(p n) k -> p (n k)", p=P))
        for c0, c1 in ((0, EARLY_CH), (EARLY_CH, NCH)):
            for sb, dr in ((o1_sb, o1), (o2_sb, o2)):
                nc.sync.dma_start(
                    out=sb[:, 4 * c0 : 4 * c1, :].rearrange("p (c n) k -> p c (n k)", n=4),
                    in_=dr[c0 * CH : c1 * CH, :].rearrange("(c p n) k -> p c (n k)", p=P, n=4),
                )
        warm = keep.tile([P, 2], F32)
        nc.vector.memset(warm[:], 0.0)
        nc.scalar.activation(out=warm[:, 1:2], in_=warm[:, 0:1], func=ACT.Relu)
        w1_sb = keep.tile([P, 4, 512], BF16)
        w2_sb = keep.tile([P, 2, 512], BF16)
        b1raw = keep.tile([P, 4], BF16)
        b2raw = keep.tile([P, 2], BF16)

        p3c = keep.tile([P, 2, 4, NT // 4, 4], BF16)
        p1 = keep.tile([P, NT, 8], BF16)
        p2 = keep.tile([P, NT, 8], BF16)
        nc.gpsimd.memset(p3c[:], 1.0)
        nc.gpsimd.memset(p1[:], 1.0)
        nc.gpsimd.memset(p2[:], 1.0)
        ident = keep.tile([P, P], F32)
        make_identity(nc, ident[:])

        nc.vector.tensor_copy(
            out=p3c[:, 0, :, :, :].rearrange("p n q t -> p q n t"),
            in_=o3_sb[:, :, 0:4].rearrange("p (q n) k -> p q n k", n=4),
        )
        nc.vector.tensor_copy(
            out=p3c[:, 1, :, :, 0:3].rearrange("p n q t -> p q n t"),
            in_=o3_sb[:, :, 4:7].rearrange("p (q n) k -> p q n k", n=4),
        )
        vts = {}
        planes = []
        for kh in range(2):
            plane = out[SCR0 + 64 * kh : SCR0 + 64 * (kh + 1), :].rearrange("r m -> (r m)")
            planes.append(plane)
            nc.sync.dma_start(
                out=plane.rearrange("(p w) -> p w", p=P),
                in_=p3c[:, kh, :, :, :].rearrange("p n q t -> p (n q t)").bitcast(F32),
            )

        nc.sync.dma_start(out=w1_sb[:], in_=We1.rearrange("(q a) k -> q a k", a=4))
        nc.sync.dma_start(out=w2_sb[:], in_=We2.rearrange("(q a) k -> q a k", a=2))
        nc.sync.dma_start(out=b1raw[:], in_=be1.rearrange("(p t) -> p t", t=4))
        nc.sync.dma_start(out=b2raw[:], in_=be2.rearrange("(q a) -> q a", a=2))

        def v_load(c0, c1):
            vt = keep.tile([P, (c1 - c0) * CH * 4], BF16, name="vt%d" % c0)
            for kh in range(2):
                nc.sync.dma_start(
                    out=vt[:].bitcast(F32)[kh:P:2, :],
                    in_=planes[kh][c0 * 1024 : c1 * 1024].partition_broadcast(64),
                )
            for c in range(c0, c1):
                vts[c] = vt[:, (c - c0) * 2048 : (c - c0 + 1) * 2048]

        for c0, c1 in V_GROUPS:
            v_load(c0, c1)

        for n0, n1 in ((0, 4 * EARLY_CH), (4 * EARLY_CH, NT)):
            nc.scalar.copy(out=p1[:, n0:n1, 0:7], in_=o1_sb[:, n0:n1, :])
            nc.scalar.copy(out=p2[:, n0:n1, 0:7], in_=o2_sb[:, n0:n1, :])

        x_nd = keep.tile([P, NT, 64], F32)
        x = keep.tile([P, NT, P], F32)

        def a1(n0, n1):
            nc.vector.tensor_tensor(
                out=x_nd[:, n0:n1, :].rearrange("p n (i j) -> p n i j", j=8),
                in0=p1[:, n0:n1, :].unsqueeze(3).to_broadcast([P, n1 - n0, 8, 8]),
                in1=p2[:, n0:n1, :].unsqueeze(2).to_broadcast([P, n1 - n0, 8, 8]),
                op=ALU.mult,
            )

        def dup(on_gpsimd, g):
            n0, n1 = 8 * g, 8 * g + 8
            dst = x[:, n0:n1, :].rearrange("p n (m d) -> p n m d", d=2)
            src = x_nd[:, n0:n1, :].unsqueeze(3).to_broadcast([P, 8, 64, 2])
            if on_gpsimd:
                nc.gpsimd.tensor_scalar(out=dst, in0=src, scalar1=1.0, scalar2=0.0, op0=ALU.mult, op1=ALU.add)
            else:
                nc.scalar.copy(out=dst, in_=src)

        def weight_tile(n_a, name):
            grouped = keep.tile([P, n_a * P * 4], BF16, align_bytes=64, name=name + "_g")
            return grouped

        def weight_pair(w_sb, grouped, n_a, ap, name):
            g_w = grouped[:].bitcast(F32).rearrange("p (a q u) -> p a q u", a=n_a, u=2)
            wt = psum.tile([P, 2, 2, P], F32, tag="r", bufs=7, name=name + "_t")
            for a2 in range(2):
                words = w_sb[:, 2 * ap + a2, :].bitcast(F32).rearrange("q (p u) -> q p u", u=2)
                for u in range(2):
                    nc.tensor.transpose(wt[:, a2, u, :], words[:, :, u], ident[:])
            nc.scalar.copy(
                out=g_w[:, 2 * ap : 2 * ap + 2, :, :],
                in_=wt[:].rearrange("p a u q -> p a q u"),
            )

        def weight_quantise(grouped, n_a, name):
            codes = keep.tile([P, n_a * P], U32, align_bytes=64, name=name + "_c")
            scales = keep.tile([P, n_a * P], U8, align_bytes=64, name=name + "_s")
            nc.vector.quantize_mx(out=codes[:].bitcast(FP8X4), scales=scales[:], in_=grouped[:])
            return codes, scales

        st = {}

        def ut(c):
            u_ps = psum.tile([P, 4, P], F32, tag="u", bufs=1)
            for n in range(4):
                nc.tensor.transpose(u_ps[:, n, :], x[:, 4 * c + n, :], ident[:])
            st[("u", c)] = u_ps

        w1g = weight_tile(4, "w1")
        w2g = weight_tile(2, "w2")
        b1 = keep.tile([P, 4], F32)
        b2 = keep.tile([P, 2], F32)
        a1(0, 16)
        dup(False, 0)
        ut(0)
        weight_pair(w1_sb, w1g, 4, 0, "w1")
        weight_pair(w1_sb, w1g, 4, 1, "w1")
        a1(16, 32)
        dup(False, 1)
        weight_pair(w2_sb, w2g, 2, 0, "w2")
        nc.scalar.copy(out=b1[:], in_=b1raw[:])
        nc.scalar.copy(out=b2[:], in_=b2raw[:])
        a1(32, 48)
        dup(False, 2)
        a1(48, 56)
        dup(True, 6)
        dup(True, 5)

        w2q = []
        w1q = []
        g0 = keep.tile([P, CH, 4], BF16, align_bytes=64, name="g0")
        g1 = keep.tile([P, CH, 4], BF16, align_bytes=64, name="g1")
        g2 = keep.tile([P, CH, 4], BF16, align_bytes=64, name="g2")
        gbuf = [g0, g1, g2]

        def relu_exit(on_vector, dst, src, bias):
            if on_vector:
                nc.vector.tensor_scalar(out=dst, in0=src, scalar1=bias, scalar2=0.0, op0=ALU.add, op1=ALU.max)
            else:
                nc.scalar.activation(out=dst, in_=src, func=ACT.Relu, bias=bias, scale=1.0)

        def copy_exit(on_vector, dst, src):
            if on_vector:
                nc.vector.tensor_copy(out=dst, in_=src)
            else:
                nc.scalar.copy(out=dst, in_=src)

        def a2(c):
            u_ps = st[("u", c)]
            fg = gbuf[c % 3]
            nc.vector.tensor_tensor(
                out=fg[:].rearrange("p (n r q) t -> p n r q t", n=4, r=8),
                in0=u_ps[:].rearrange("p n (r q) -> p n r q", r=8).unsqueeze(4).to_broadcast([P, 4, 8, 16, 4]),
                in1=vts[c].rearrange("p (r n q t) -> p n r q t", r=8, n=4, t=4),
                op=ALU.mult,
            )
            st[("fg", c)] = fg

        def quantise(key_in, key_out, c):
            src = st[(key_in, c)]
            codes = work.tile([P, CH], U32, align_bytes=64, name=key_out + "c")
            scales = work.tile([P, CH], U8, align_bytes=64, name=key_out + "s")
            nc.vector.quantize_mx(
                out=codes[:].bitcast(FP8X4), scales=scales[:], in_=src[:].rearrange("p c t -> p (c t)")
            )
            st[(key_out, c)] = (codes, scales)

        def l1(c, t):
            fc, fs = st[("f", c)]
            hp = psum.tile([P, CH], F32, tag="r", bufs=7)
            nc.tensor.matmul_mx(
                out=hp[:],
                lhsT=w1q[0][:, t * P : (t + 1) * P].bitcast(FP8X4),
                lhsT_scale=w1q[1][:, t * P : (t + 1) * P],
                rhs=fc[:].bitcast(FP8X4),
                rhs_scale=fs[:],
                start=True,
                stop=True,
            )
            st[("hp", c, t)] = hp

        def c1(c, t):
            if t == 0:
                h_new = work.tile([P, 4, CH], BF16, name="h", bufs=3)
                st[("h", c)] = h_new
            h = st[("h", c)]
            relu_exit(c == NCH - 1 and t >= 2, h[:, t, :], st[("hp", c, t)][:], b1[:, t : t + 1])

        def c2(c):
            h = st[("h", c)]
            hg = gbuf[(c + 1) % 3]
            if c >= NCH - TAIL_D:
                nc.vector.tensor_copy(
                    out=hg[:].rearrange("p (c i) t -> p c t i", i=4),
                    in_=h[:].rearrange("p t (c i) -> p c t i", i=4),
                )
            else:
                nc.gpsimd.tensor_scalar(
                    out=hg[:],
                    in0=h[:].rearrange("p t c -> p c t"),
                    scalar1=1.0,
                    scalar2=0.0,
                    op0=ALU.mult,
                    op1=ALU.add,
                )
            st[("hg", c)] = hg

        def l2(c):
            hc, hs = st[("hq", c)]
            for a in range(2):
                o2p = psum.tile([P, CH], F32, tag="r", bufs=7)
                nc.tensor.matmul_mx(
                    out=o2p[:],
                    lhsT=w2q[0][:, a * P : (a + 1) * P].bitcast(FP8X4),
                    lhsT_scale=w2q[1][:, a * P : (a + 1) * P],
                    rhs=hc[:].bitcast(FP8X4),
                    rhs_scale=hs[:],
                    start=True,
                    stop=True,
                )
                st[("o2", c, a)] = o2p

        def e1(c):
            ot = work.tile([P, 2, CH], F32)
            for a in range(2):
                relu_exit(c >= TAIL_X and a == 1, ot[:, a, :], st[("o2", c, a)][:], b2[:, a : a + 1])
            st[("ot", c)] = ot

        def et(c, sp):
            ot = st[("ot", c)]
            otr = psum.tile([P, 2, 2, P], F32, tag="r", bufs=7)
            for s2 in range(2):
                s = 2 * sp + s2
                for a in range(2):
                    nc.tensor.transpose(otr[:, s2, a, :], ot[:, a, s * P : (s + 1) * P], ident[:])
            st[("otr", c, sp)] = otr

        def e2(c, sp):
            if ("o", c) not in st:
                o_new = work.tile([P, 4, M], F32, bufs=OUT_BUFS, name="o_sb")
                st[("o", c)] = o_new
            o_sb = st[("o", c)]
            copy_exit(
                sp == 0,
                o_sb[:, 2 * sp : 2 * sp + 2, :].rearrange("p s (q a) -> p s q a", a=2),
                st[("otr", c, sp)][:].rearrange("p s a q -> p s q a"),
            )
            nc.sync.dma_start(
                out=out[c * CH : (c + 1) * CH, :].rearrange("(r s) m -> r s m", s=4)[:, 2 * sp : 2 * sp + 2, :],
                in_=o_sb[:, 2 * sp : 2 * sp + 2, :],
            )

        def live(c):
            return 0 <= c < NCH

        for k in range(NCH + 5):
            if live(k):
                a2(k)
            if live(k + 1):
                ut(k + 1)
            if live(k - 4) and live(k):
                e2(k - 4, 0)
            if k == 0:
                w1q.extend(weight_quantise(w1g, 4, "w1"))
            if live(k):
                quantise("fg", "f", k)
            if k == 0:
                w2q.extend(weight_quantise(w2g, 2, "w2"))
                a1(56, 64)
                dup(True, 7)
            if live(k - 2) and k <= NCH:
                quantise("hg", "hq", k - 2)
            if live(k - 1):
                c2(k - 1)
            if live(k - 4) and not live(k):
                e2(k - 4, 0)
            if k == NCH:
                quantise("hg", "hq", k - 1)
            if live(k):
                for t in range(3):
                    l1(k, t)
                c1(k, 0)
                if live(k - 3):
                    et(k - 3, 0)
                l1(k, 3)
            if live(k - 2):
                l2(k - 2)
            if live(k - 3):
                if not live(k):
                    et(k - 3, 0)
                et(k - 3, 1)
            if live(k):
                for t in range(1, 4):
                    c1(k, t)
            if live(k - 2):
                e1(k - 2)
            if live(k - 3):
                e2(k - 3, 1)
            if k < 2:
                dup(False, 3 + k)
